import numpy as np
import ml_dtypes


def mxq(x, axis, fmt="e4m3"):
    dtype, down = {"e4m3": (ml_dtypes.float8_e4m3fn, 7), "e5m2": (ml_dtypes.float8_e5m2, 14)}[fmt]
    v = np.moveaxis(np.asarray(x, np.float32).astype(ml_dtypes.bfloat16).astype(np.float64), axis, -1)
    blocks = v.reshape(v.shape[:-1] + (-1, 32))
    amax = np.abs(blocks).max(-1, keepdims=True)
    byte = np.maximum(np.where(amax > 0, np.frexp(amax)[1] - 1 + 127, 0) - down, 1)
    scale = np.exp2(byte - 127.0)
    codes = (blocks / scale).astype(np.float32).astype(dtype).astype(np.float64)
    return np.moveaxis((codes * scale).reshape(v.shape), -1, axis)


WIDE = False


def mx_kscale(k):
    if not WIDE:
        return np.ones(k)
    levels = np.array([10, -10, 5, -5, 0])
    if k % 512:
        return np.exp2(np.random.permutation(np.resize(levels, k // 32))).repeat(32)
    a = np.empty((k // 512, 16))
    for p in range(k // 512):
        a[p, :8] = np.random.permutation(np.resize(levels, 8))
        for g in range(8):
            far = levels[np.abs(levels - a[p, g]) >= 10]
            a[p, g + 8] = far[np.random.randint(len(far))]
    return np.exp2(a.ravel()).repeat(32)


BF16 = ml_dtypes.bfloat16


def bf(x):
    return np.asarray(x, np.float32).astype(BF16)


def f64(x):
    return np.asarray(x).astype(np.float64)


B, C, HH, WW = 1, 512, 32, 32
N = HH * WW


def setup_inputs():
    s, t = mx_kscale(C), mx_kscale(C)
    return {"x": bf(np.random.standard_normal((B, C, HH, WW)) * s[None, :, None, None]),
            "Wq": bf(np.random.standard_normal((C, C)) * 1.4 / np.sqrt(C) * t[:, None] / s[None, :]),
            "bq": bf(np.random.standard_normal(C) * 0.2 * t),
            "k": bf(np.random.standard_normal((B, N, C)) * 1.4 / t)}


def reference(x, Wq, bq, k):
    xt = f64(x).reshape(B, C, N)
    q = (mxq(xt, 1, "e4m3").transpose(0, 2, 1) @ mxq(f64(Wq), 1, "e4m3").T) + f64(bq)
    scores = mxq(q / np.sqrt(C), 2, "e4m3") @ mxq(f64(k), 2, "e4m3").transpose(0, 2, 1)
    e = np.exp(scores - scores.max(-1, keepdims=True))
    return e / e.sum(-1, keepdims=True)

@@ -1,0 +1,288 @@
+from contextlib import ExitStack
+import math
+
+import concourse.mybir as mybir
+from concourse.masks import make_identity
+
+F32 = mybir.dt.float32
+BF16 = mybir.dt.bfloat16
+U32 = mybir.dt.uint32
+U8 = mybir.dt.uint8
+FP8X4 = mybir.dt.float8_e4m3fn_x4
+ALU = mybir.AluOpType
+ACT = mybir.ActivationFunctionType
+AX = mybir.AxisListType
+
+P = 128
+C = 512
+NTOK = 1024
+NT = NTOK // P
+QBANK = F32
+
+FLOPS = 2 * NTOK * C * C + 2 * NTOK * NTOK * C
+
+X_CHUNKS = (256, 256, 512)
+PRE_K = 3
+V_TAIL = 2
+
+
+def tile_visionattention_pa_kernel(tc, x, Wq, bq, k, out):
+    nc = tc.nc
+    inv_sqrt_c = 1.0 / math.sqrt(C)
+
+    with ExitStack() as ctx:
+        const = ctx.enter_context(tc.tile_pool(name="const", bufs=1))
+        keep = ctx.enter_context(tc.tile_pool(name="keep", bufs=1))
+        soft = ctx.enter_context(tc.tile_pool(name="soft", bufs=5))
+        stat = ctx.enter_context(tc.tile_pool(name="stat", bufs=5))
+        psum = ctx.enter_context(tc.psum_pool(name="psum", bufs=8))
+        ctx.enter_context(tc.manual_schedule())
+
+        bq_raw = const.tile([P, 4], BF16, name="bq_raw")
+        nc.scalar.dma_start(out=bq_raw[:], in_=bq.rearrange("(p t) -> p t", t=4))
+
+        w_view = Wq.rearrange("(m t) c -> m t c", t=4)
+        x_view = x[0].rearrange("(p j) h w -> p j (h w)", j=4)
+        k_view = k[0].rearrange("(a p) c -> p a c", p=P)
+        w_raw = []
+        x_raw = []
+        k_raw = []
+
+        def load_w(b):
+            wr = keep.tile([P, 2, C], BF16, name="w_raw%d" % b)
+            nc.sync.dma_start(out=wr[:], in_=w_view[:, 2 * b : 2 * b + 2, :])
+            w_raw.append(wr)
+
+        def load_x(c):
+            n0 = sum(X_CHUNKS[:c])
+            xr = keep.tile([P, 4, X_CHUNKS[c]], BF16, name="x_raw%d" % c)
+            nc.sync.dma_start(out=xr[:], in_=x_view[:, :, n0 : n0 + X_CHUNKS[c]])
+            x_raw.append(xr)
+
+        def load_k(g):
+            kr = keep.tile([P, 2, C], BF16, name="k_raw%d" % g)
+            nc.sync.dma_start(out=kr[:], in_=k_view[:, 2 * g : 2 * g + 2, :])
+            k_raw.append(kr)
+
+        load_w(0)
+        load_w(1)
+        load_x(0)
+        for g in range(4):
+            load_k(g)
+        load_x(1)
+        load_x(2)
+
+        ident = const.tile([P, P], F32, name="ident")
+        make_identity(nc, ident[:])
+        warm_in = const.tile([P, 1], F32, name="warm_in")
+        warm_out = const.tile([P, 1], F32, name="warm_out")
+        nc.vector.memset(warm_in[:], 0.0)
+        nc.scalar.activation(out=warm_out[:], in_=warm_in[:], func=ACT.Exp)
+        bias_s = const.tile([P, 4], F32, name="bias_s")
+
+        def turn(raw, grp_words, name):
+            words = raw[:].rearrange("r s c -> r (s c)").bitcast(F32)
+            bank = psum.tile([P, 2, 2, P], F32, tag="bank", name=name)
+            for s in range(2):
+                for u in range(2):
+                    nc.tensor.transpose(bank[:, s, u, :], words[:, 256 * s + u : 256 * (s + 1) : 2], ident[:])
+            nc.scalar.copy(
+                out=grp_words.rearrange("p (s r u) -> p s r u", s=2, u=2),
+                in_=bank[:].rearrange("p s u r -> p s r u"),
+            )
+
+        w_grp = keep.tile([P, 4 * C], BF16, name="w_grp", align_bytes=64)
+        w_codes = keep.tile([P, C], U32, name="w_codes", align_bytes=64)
+        w_scales = keep.tile([P, C], U8, name="w_scales", align_bytes=64)
+        w_grp_words = w_grp[:].bitcast(F32)
+
+        x_grp = []
+        x_codes = []
+        x_scales = []
+
+        def group_x(c, engine):
+            xg = keep.tile([P, X_CHUNKS[c], 4], BF16, name="x_grp%d" % c, align_bytes=64)
+            src = x_raw[c][:].rearrange("p j n -> p n j")
+            if engine == "scalar":
+                nc.scalar.copy(out=xg[:], in_=src)
+            else:
+                nc.vector.tensor_copy(out=xg[:], in_=src)
+            x_grp.append(xg)
+
+        def quant_x(c):
+            xc = keep.tile([P, X_CHUNKS[c]], U32, name="x_codes%d" % c, align_bytes=64)
+            xs = keep.tile([P, X_CHUNKS[c]], U8, name="x_scales%d" % c, align_bytes=64)
+            nc.vector.quantize_mx(out=xc[:].bitcast(FP8X4), scales=xs[:], in_=x_grp[c][:].rearrange("p n j -> p (n j)"))
+            x_codes.append(xc)
+            x_scales.append(xs)
+
+        k_grp = []
+        for h in range(2):
+            kg = keep.tile([P, 4 * C], BF16, name="k_grp%d" % h, align_bytes=64)
+            k_grp.append(kg)
+        k_codes = []
+        k_scales = []
+
+        def turn_k(g):
+            turn(k_raw[g], k_grp[g // 2][:].bitcast(F32)[:, 512 * (g % 2) : 512 * (g % 2 + 1)], "kt%d" % g)
+
+        def quant_k(h):
+            kc = keep.tile([P, C], U32, name="k_codes%d" % h, align_bytes=64)
+            ks = keep.tile([P, C], U8, name="k_scales%d" % h, align_bytes=64)
+            nc.vector.quantize_mx(out=kc[:].bitcast(FP8X4), scales=ks[:], in_=k_grp[h][:])
+            k_codes.append(kc)
+            k_scales.append(ks)
+
+        chunk_of = []
+        for c in range(len(X_CHUNKS)):
+            for j in range(X_CHUNKS[c] // P):
+                chunk_of.append((c, j))
+
+        q_bank = {}
+        q_grp = {}
+        q_codes = {}
+        q_scales = {}
+
+        def project(i):
+            c, j = chunk_of[i]
+            qp = psum.tile([P, 4, P], QBANK, tag="bank", name="qp")
+            for t in range(4):
+                nc.tensor.matmul_mx(
+                    out=qp[:, t, :],
+                    lhsT=w_codes[:, P * t : P * (t + 1)].bitcast(FP8X4),
+                    lhsT_scale=w_scales[:, P * t : P * (t + 1)],
+                    rhs=x_codes[c][:, P * j : P * (j + 1)].bitcast(FP8X4),
+                    rhs_scale=x_scales[c][:, P * j : P * (j + 1)],
+                    start=True,
+                    stop=True,
+                )
+            q_bank[i] = qp
+
+        def read_q(i):
+            qg = keep.tile([P, P, 4], BF16, name="q_grp%d" % i, align_bytes=64)
+            nc.vector.scalar_tensor_tensor(
+                out=qg[:],
+                in0=q_bank[i][:].rearrange("p t n -> p n t"),
+                scalar=inv_sqrt_c,
+                in1=bias_s[:].unsqueeze(1).to_broadcast([P, P, 4]),
+                op0=ALU.mult,
+                op1=ALU.add,
+            )
+            q_grp[i] = qg
+
+        def quant_q(i):
+            qc = keep.tile([P, P], U32, name="q_codes%d" % i, align_bytes=64)
+            qs = keep.tile([P, P], U8, name="q_scales%d" % i, align_bytes=64)
+            nc.vector.quantize_mx(out=qc[:].bitcast(FP8X4), scales=qs[:], in_=q_grp[i][:].rearrange("p n t -> p (n t)"))
+            q_codes[i] = qc
+            q_scales[i] = qs
+
+        sc = {}
+        mx = {}
+        nmax = {}
+        ex = {}
+        ssum = {}
+        tot = {}
+
+        def scores(i):
+            pair = []
+            for h in range(2):
+                s_h = psum.tile([P, C], F32, tag="bank", name="sc%d" % h)
+                nc.tensor.matmul_mx(
+                    out=s_h[:],
+                    lhsT=q_codes[i][:].bitcast(FP8X4),
+                    lhsT_scale=q_scales[i][:],
+                    rhs=k_codes[h][:].bitcast(FP8X4),
+                    rhs_scale=k_scales[h][:],
+                    start=True,
+                    stop=True,
+                )
+                pair.append(s_h)
+            sc[i] = pair
+
+        def half_maxima(i):
+            m = stat.tile([P, 2], F32, name="mx")
+            for h in range(2):
+                nc.vector.tensor_reduce(out=m[:, h : h + 1], in_=sc[i][h][:], axis=AX.X, op=ALU.max)
+            mx[i] = m
+
+        def exponentials(i):
+            nm = stat.tile([P, 1], F32, name="nmax")
+            nc.vector.tensor_scalar(out=nm[:], in0=mx[i][:, 0:1], scalar1=mx[i][:, 1:2], scalar2=-1.0, op0=ALU.max, op1=ALU.mult)
+            e = soft.tile([P, NTOK], F32, name="e")
+            s2 = stat.tile([P, 2], F32, name="ssum")
+            for h in range(2):
+                nc.scalar.activation(
+                    out=e[:, C * h : C * (h + 1)],
+                    in_=sc[i][h][:],
+                    func=ACT.Exp,
+                    bias=nm[:],
+                    scale=1.0,
+                    accum_out=s2[:, h : h + 1],
+                )
+            ex[i] = e
+            ssum[i] = s2
+
+        def row_sum(i):
+            t = stat.tile([P, 1], F32, name="tot")
+            nc.vector.tensor_reduce(out=t[:], in_=ssum[i][:], axis=AX.X, op=ALU.add)
+            tot[i] = t
+
+        def finish(i):
+            rinv = stat.tile([P, 1], F32, name="rinv")
+            nc.vector.reciprocal(out=rinv[:], in_=tot[i][:])
+            o = soft.tile([P, NTOK], F32, name="o")
+            for h in range(2):
+                cols = slice(C * h, C * (h + 1))
+                if i >= NT - V_TAIL:
+                    nc.vector.tensor_scalar(out=o[:, cols], in0=ex[i][:, cols], scalar1=rinv[:], scalar2=None, op0=ALU.mult)
+                else:
+                    nc.gpsimd.tensor_scalar(out=o[:, cols], in0=ex[i][:, cols], scalar1=rinv[:], scalar2=0.0, op0=ALU.mult, op1=ALU.add)
+                nc.sync.dma_start(out=out[0, P * i : P * (i + 1), cols], in_=o[:, cols])
+
+        turn(w_raw[0], w_grp_words[:, 0:512], "wt0")
+        turn(w_raw[1], w_grp_words[:, 512:1024], "wt1")
+        group_x(0, "vector")
+        nc.vector.quantize_mx(out=w_codes[:].bitcast(FP8X4), scales=w_scales[:], in_=w_grp[:])
+        quant_x(0)
+        nc.vector.tensor_scalar(out=bias_s[:], in0=bq_raw[:], scalar1=inv_sqrt_c, scalar2=None, op0=ALU.mult)
+        for g in range(PRE_K):
+            turn_k(g)
+        project(0)
+        project(1)
+        for g in range(PRE_K, 4):
+            turn_k(g)
+        group_x(1, "scalar")
+        group_x(2, "scalar")
+        quant_k(0)
+        read_q(0)
+        read_q(1)
+        quant_q(0)
+        quant_k(1)
+        scores(0)
+        quant_q(1)
+        quant_x(1)
+        project(2)
+        scores(1)
+
+        for i in range(NT + 1):
+            if i < NT:
+                half_maxima(i)
+            if i + 2 < NT:
+                read_q(i + 2)
+                exponentials(i)
+                if i >= 1:
+                    row_sum(i - 1)
+                if i + 3 == 4:
+                    quant_x(2)
+                if i + 3 < NT:
+                    project(i + 3)
+                quant_q(i + 2)
+                scores(i + 2)
+                if i >= 1:
+                    finish(i - 1)
+            else:
+                row_sum(i - 1)
+                if i < NT:
+                    exponentials(i)
+                finish(i - 1)

@@ -22,8 +22,8 @@ QBANK = F32
 FLOPS = 2 * NTOK * C * C + 2 * NTOK * NTOK * C
 
 X_CHUNKS = (256, 256, 512)
-PRE_K = 3
-V_TAIL = 2
+AHEAD = 3
+V_TAIL = 3
 
 
 def tile_visionattention_pa_kernel(tc, x, Wq, bq, k, out):
@@ -34,7 +34,7 @@ def tile_visionattention_pa_kernel(tc, x, Wq, bq, k, out):
         const = ctx.enter_context(tc.tile_pool(name="const", bufs=1))
         keep = ctx.enter_context(tc.tile_pool(name="keep", bufs=1))
         soft = ctx.enter_context(tc.tile_pool(name="soft", bufs=5))
-        stat = ctx.enter_context(tc.tile_pool(name="stat", bufs=5))
+        stat = ctx.enter_context(tc.tile_pool(name="stat", bufs=6))
         psum = ctx.enter_context(tc.psum_pool(name="psum", bufs=8))
         ctx.enter_context(tc.manual_schedule())
 
@@ -43,33 +43,32 @@ def tile_visionattention_pa_kernel(tc, x, Wq, bq, k, out):
 
         w_view = Wq.rearrange("(m t) c -> m t c", t=4)
         x_view = x[0].rearrange("(p j) h w -> p j (h w)", j=4)
-        k_view = k[0].rearrange("(a p) c -> p a c", p=P)
-        w_raw = []
-        x_raw = []
-        k_raw = []
+        k_view = k[0].rearrange("(g r b) c -> r g b c", r=P, b=2)
+        w_raw = {}
+        x_raw = {}
+        k_raw = {}
 
         def load_w(b):
-            wr = keep.tile([P, 2, C], BF16, name="w_raw%d" % b)
-            nc.sync.dma_start(out=wr[:], in_=w_view[:, 2 * b : 2 * b + 2, :])
-            w_raw.append(wr)
+            w_raw[b] = keep.tile([P, 2, C], BF16, name="w_raw%d" % b)
+            nc.sync.dma_start(out=w_raw[b][:], in_=w_view[:, 2 * b : 2 * b + 2, :])
 
         def load_x(c):
             n0 = sum(X_CHUNKS[:c])
-            xr = keep.tile([P, 4, X_CHUNKS[c]], BF16, name="x_raw%d" % c)
-            nc.sync.dma_start(out=xr[:], in_=x_view[:, :, n0 : n0 + X_CHUNKS[c]])
-            x_raw.append(xr)
+            x_raw[c] = keep.tile([P, 4, X_CHUNKS[c]], BF16, name="x_raw%d" % c)
+            nc.sync.dma_start(out=x_raw[c][:], in_=x_view[:, :, n0 : n0 + X_CHUNKS[c]])
 
         def load_k(g):
-            kr = keep.tile([P, 2, C], BF16, name="k_raw%d" % g)
-            nc.sync.dma_start(out=kr[:], in_=k_view[:, 2 * g : 2 * g + 2, :])
-            k_raw.append(kr)
+            k_raw[g] = keep.tile([P, 2, C], BF16, name="k_raw%d" % g)
+            nc.sync.dma_start(out=k_raw[g][:], in_=k_view[:, g, :, :])
 
         load_w(0)
         load_w(1)
+        load_k(0)
         load_x(0)
-        for g in range(4):
-            load_k(g)
+        load_k(1)
+        load_k(2)
         load_x(1)
+        load_k(3)
         load_x(2)
 
         ident = const.tile([P, P], F32, name="ident")
@@ -80,58 +79,61 @@ def tile_visionattention_pa_kernel(tc, x, Wq, bq, k, out):
         nc.scalar.activation(out=warm_out[:], in_=warm_in[:], func=ACT.Exp)
         bias_s = const.tile([P, 4], F32, name="bias_s")
 
-        def turn(raw, grp_words, name):
+        def turn(raw, name):
             words = raw[:].rearrange("r s c -> r (s c)").bitcast(F32)
             bank = psum.tile([P, 2, 2, P], F32, tag="bank", name=name)
             for s in range(2):
                 for u in range(2):
                     nc.tensor.transpose(bank[:, s, u, :], words[:, 256 * s + u : 256 * (s + 1) : 2], ident[:])
-            nc.scalar.copy(
-                out=grp_words.rearrange("p (s r u) -> p s r u", s=2, u=2),
-                in_=bank[:].rearrange("p s u r -> p s r u"),
-            )
+            return bank
 
         w_grp = keep.tile([P, 4 * C], BF16, name="w_grp", align_bytes=64)
         w_codes = keep.tile([P, C], U32, name="w_codes", align_bytes=64)
         w_scales = keep.tile([P, C], U8, name="w_scales", align_bytes=64)
-        w_grp_words = w_grp[:].bitcast(F32)
 
-        x_grp = []
-        x_codes = []
-        x_scales = []
+        def turn_w(b):
+            bank = turn(w_raw[b], "wt%d" % b)
+            nc.scalar.copy(
+                out=w_grp[:].bitcast(F32)[:, 512 * b : 512 * (b + 1)].rearrange("p (s r u) -> p s r u", s=2, u=2),
+                in_=bank[:].rearrange("p s u r -> p s r u"),
+            )
+
+        x_grp = {}
+        x_codes = {}
+        x_scales = {}
 
         def group_x(c, engine):
-            xg = keep.tile([P, X_CHUNKS[c], 4], BF16, name="x_grp%d" % c, align_bytes=64)
+            x_grp[c] = keep.tile([P, X_CHUNKS[c], 4], BF16, name="x_grp%d" % c, align_bytes=64)
             src = x_raw[c][:].rearrange("p j n -> p n j")
             if engine == "scalar":
-                nc.scalar.copy(out=xg[:], in_=src)
+                nc.scalar.copy(out=x_grp[c][:], in_=src)
             else:
-                nc.vector.tensor_copy(out=xg[:], in_=src)
-            x_grp.append(xg)
+                nc.vector.tensor_copy(out=x_grp[c][:], in_=src)
 
         def quant_x(c):
-            xc = keep.tile([P, X_CHUNKS[c]], U32, name="x_codes%d" % c, align_bytes=64)
-            xs = keep.tile([P, X_CHUNKS[c]], U8, name="x_scales%d" % c, align_bytes=64)
-            nc.vector.quantize_mx(out=xc[:].bitcast(FP8X4), scales=xs[:], in_=x_grp[c][:].rearrange("p n j -> p (n j)"))
-            x_codes.append(xc)
-            x_scales.append(xs)
+            x_codes[c] = keep.tile([P, X_CHUNKS[c]], U32, name="x_codes%d" % c, align_bytes=64)
+            x_scales[c] = keep.tile([P, X_CHUNKS[c]], U8, name="x_scales%d" % c, align_bytes=64)
+            nc.vector.quantize_mx(
+                out=x_codes[c][:].bitcast(FP8X4), scales=x_scales[c][:], in_=x_grp[c][:].rearrange("p n j -> p (n j)")
+            )
 
-        k_grp = []
+        k_grp = {}
         for h in range(2):
-            kg = keep.tile([P, 4 * C], BF16, name="k_grp%d" % h, align_bytes=64)
-            k_grp.append(kg)
-        k_codes = []
-        k_scales = []
+            k_grp[h] = keep.tile([P, 4 * C], BF16, name="k_grp%d" % h, align_bytes=64)
+        k_codes = {}
+        k_scales = {}
 
         def turn_k(g):
-            turn(k_raw[g], k_grp[g // 2][:].bitcast(F32)[:, 512 * (g % 2) : 512 * (g % 2 + 1)], "kt%d" % g)
+            bank = turn(k_raw[g], "kt%d" % g)
+            nc.scalar.copy(
+                out=k_grp[g // 2][:].bitcast(F32)[:, 512 * (g % 2) : 512 * (g % 2 + 1)].rearrange("p (r q) -> p r q", q=4),
+                in_=bank[:].rearrange("p b u r -> p r (b u)"),
+            )
 
         def quant_k(h):
-            kc = keep.tile([P, C], U32, name="k_codes%d" % h, align_bytes=64)
-            ks = keep.tile([P, C], U8, name="k_scales%d" % h, align_bytes=64)
-            nc.vector.quantize_mx(out=kc[:].bitcast(FP8X4), scales=ks[:], in_=k_grp[h][:])
-            k_codes.append(kc)
-            k_scales.append(ks)
+            k_codes[h] = keep.tile([P, C], U32, name="k_codes%d" % h, align_bytes=64)
+            k_scales[h] = keep.tile([P, C], U8, name="k_scales%d" % h, align_bytes=64)
+            nc.vector.quantize_mx(out=k_codes[h][:].bitcast(FP8X4), scales=k_scales[h][:], in_=k_grp[h][:])
 
         chunk_of = []
         for c in range(len(X_CHUNKS)):
@@ -145,10 +147,12 @@ def tile_visionattention_pa_kernel(tc, x, Wq, bq, k, out):
 
         def project(i):
             c, j = chunk_of[i]
-            qp = psum.tile([P, 4, P], QBANK, tag="bank", name="qp")
+            if c not in x_codes:
+                quant_x(c)
+            q_bank[i] = psum.tile([P, 4, P], QBANK, tag="bank", name="qp")
             for t in range(4):
                 nc.tensor.matmul_mx(
-                    out=qp[:, t, :],
+                    out=q_bank[i][:, t, :],
                     lhsT=w_codes[:, P * t : P * (t + 1)].bitcast(FP8X4),
                     lhsT_scale=w_scales[:, P * t : P * (t + 1)],
                     rhs=x_codes[c][:, P * j : P * (j + 1)].bitcast(FP8X4),
@@ -156,36 +160,33 @@ def tile_visionattention_pa_kernel(tc, x, Wq, bq, k, out):
                     start=True,
                     stop=True,
                 )
-            q_bank[i] = qp
 
         def read_q(i):
-            qg = keep.tile([P, P, 4], BF16, name="q_grp%d" % i, align_bytes=64)
+            q_grp[i] = keep.tile([P, P, 4], BF16, name="q_grp%d" % i, align_bytes=64)
             nc.vector.scalar_tensor_tensor(
-                out=qg[:],
+                out=q_grp[i][:],
                 in0=q_bank[i][:].rearrange("p t n -> p n t"),
                 scalar=inv_sqrt_c,
                 in1=bias_s[:].unsqueeze(1).to_broadcast([P, P, 4]),
                 op0=ALU.mult,
                 op1=ALU.add,
             )
-            q_grp[i] = qg
 
         def quant_q(i):
-            qc = keep.tile([P, P], U32, name="q_codes%d" % i, align_bytes=64)
-            qs = keep.tile([P, P], U8, name="q_scales%d" % i, align_bytes=64)
-            nc.vector.quantize_mx(out=qc[:].bitcast(FP8X4), scales=qs[:], in_=q_grp[i][:].rearrange("p n t -> p (n t)"))
-            q_codes[i] = qc
-            q_scales[i] = qs
+            q_codes[i] = keep.tile([P, P], U32, name="q_codes%d" % i, align_bytes=64)
+            q_scales[i] = keep.tile([P, P], U8, name="q_scales%d" % i, align_bytes=64)
+            nc.vector.quantize_mx(
+                out=q_codes[i][:].bitcast(FP8X4), scales=q_scales[i][:], in_=q_grp[i][:].rearrange("p n t -> p (n t)")
+            )
 
         sc = {}
         mx = {}
-        nmax = {}
         ex = {}
         ssum = {}
         tot = {}
 
         def scores(i):
-            pair = []
+            sc[i] = []
             for h in range(2):
                 s_h = psum.tile([P, C], F32, tag="bank", name="sc%d" % h)
                 nc.tensor.matmul_mx(
@@ -197,36 +198,33 @@ def tile_visionattention_pa_kernel(tc, x, Wq, bq, k, out):
                     start=True,
                     stop=True,
                 )
-                pair.append(s_h)
-            sc[i] = pair
+                sc[i].append(s_h)
 
-        def half_maxima(i):
-            m = stat.tile([P, 2], F32, name="mx")
-            for h in range(2):
-                nc.vector.tensor_reduce(out=m[:, h : h + 1], in_=sc[i][h][:], axis=AX.X, op=ALU.max)
-            mx[i] = m
+        def bank_max(i, h):
+            if h == 0:
+                mx[i] = stat.tile([P, 2], F32, name="mx")
+            nc.vector.tensor_reduce(out=mx[i][:, h : h + 1], in_=sc[i][h][:], axis=AX.X, op=ALU.max)
 
         def exponentials(i):
             nm = stat.tile([P, 1], F32, name="nmax")
-            nc.vector.tensor_scalar(out=nm[:], in0=mx[i][:, 0:1], scalar1=mx[i][:, 1:2], scalar2=-1.0, op0=ALU.max, op1=ALU.mult)
-            e = soft.tile([P, NTOK], F32, name="e")
-            s2 = stat.tile([P, 2], F32, name="ssum")
+            nc.vector.tensor_scalar(
+                out=nm[:], in0=mx[i][:, 0:1], scalar1=mx[i][:, 1:2], scalar2=-1.0, op0=ALU.max, op1=ALU.mult
+            )
+            ex[i] = soft.tile([P, NTOK], F32, name="e")
+            ssum[i] = stat.tile([P, 2], F32, name="ssum")
             for h in range(2):
                 nc.scalar.activation(
-                    out=e[:, C * h : C * (h + 1)],
+                    out=ex[i][:, C * h : C * (h + 1)],
                     in_=sc[i][h][:],
                     func=ACT.Exp,
                     bias=nm[:],
                     scale=1.0,
-                    accum_out=s2[:, h : h + 1],
+                    accum_out=ssum[i][:, h : h + 1],
                 )
-            ex[i] = e
-            ssum[i] = s2
 
         def row_sum(i):
-            t = stat.tile([P, 1], F32, name="tot")
-            nc.vector.tensor_reduce(out=t[:], in_=ssum[i][:], axis=AX.X, op=ALU.add)
-            tot[i] = t
+            tot[i] = stat.tile([P, 1], F32, name="tot")
+            nc.vector.tensor_reduce(out=tot[i][:], in_=ssum[i][:], axis=AX.X, op=ALU.add)
 
         def finish(i):
             rinv = stat.tile([P, 1], F32, name="rinv")
@@ -237,52 +235,70 @@ def tile_visionattention_pa_kernel(tc, x, Wq, bq, k, out):
                 if i >= NT - V_TAIL:
                     nc.vector.tensor_scalar(out=o[:, cols], in0=ex[i][:, cols], scalar1=rinv[:], scalar2=None, op0=ALU.mult)
                 else:
-                    nc.gpsimd.tensor_scalar(out=o[:, cols], in0=ex[i][:, cols], scalar1=rinv[:], scalar2=0.0, op0=ALU.mult, op1=ALU.add)
+                    nc.gpsimd.tensor_scalar(
+                        out=o[:, cols], in0=ex[i][:, cols], scalar1=rinv[:], scalar2=0.0, op0=ALU.mult, op1=ALU.add
+                    )
                 nc.sync.dma_start(out=out[0, P * i : P * (i + 1), cols], in_=o[:, cols])
 
-        turn(w_raw[0], w_grp_words[:, 0:512], "wt0")
-        turn(w_raw[1], w_grp_words[:, 512:1024], "wt1")
+        turn_w(0)
+        turn_w(1)
         group_x(0, "vector")
         nc.vector.quantize_mx(out=w_codes[:].bitcast(FP8X4), scales=w_scales[:], in_=w_grp[:])
         quant_x(0)
         nc.vector.tensor_scalar(out=bias_s[:], in0=bq_raw[:], scalar1=inv_sqrt_c, scalar2=None, op0=ALU.mult)
-        for g in range(PRE_K):
-            turn_k(g)
-        project(0)
-        project(1)
-        for g in range(PRE_K, 4):
-            turn_k(g)
+        turn_k(0)
+        turn_k(1)
+        turn_k(2)
         group_x(1, "scalar")
-        group_x(2, "scalar")
+        project(0)
         quant_k(0)
+        project(1)
         read_q(0)
         read_q(1)
         quant_q(0)
+        quant_x(1)
+        turn_k(3)
+        quant_q(1)
+        project(2)
+        group_x(2, "scalar")
         quant_k(1)
         scores(0)
-        quant_q(1)
-        quant_x(1)
-        project(2)
         scores(1)
+        read_q(2)
 
-        for i in range(NT + 1):
-            if i < NT:
-                half_maxima(i)
-            if i + 2 < NT:
-                read_q(i + 2)
-                exponentials(i)
-                if i >= 1:
-                    row_sum(i - 1)
-                if i + 3 == 4:
-                    quant_x(2)
-                if i + 3 < NT:
-                    project(i + 3)
-                quant_q(i + 2)
-                scores(i + 2)
-                if i >= 1:
-                    finish(i - 1)
-            else:
-                row_sum(i - 1)
-                if i < NT:
+        big = []
+        for i in range(NT):
+            big.append(("max", i, 0))
+            big.append(("max", i, 1))
+            if i + AHEAD < NT:
+                big.append(("read_q", i + AHEAD, 0))
+        pending = [(1, 1, AHEAD - 1)]
+        done = 0
+        while done < len(big) or pending:
+            if done < len(big):
+                kind, i, h = big[done]
+                if kind == "max":
+                    if h == 0 and i + AHEAD < NT:
+                        project(i + AHEAD)
+                    bank_max(i, h)
+                    if h == 1:
+                        pending.append((done + 2, 0, i))
+                else:
+                    read_q(i)
+                    pending.append((done + 2, 1, i))
+            done += 1
+            ready = sorted(p for p in pending if p[0] <= done)
+            ready = sorted(ready, key=lambda p: (p[1], p[2]))
+            pending = [p for p in pending if p[0] > done]
+            for due, rank, i in ready:
+                if rank == 0:
                     exponentials(i)
-                finish(i - 1)
+                    pending.append((done + 3, 2, i))
+                elif rank == 1:
+                    quant_q(i)
+                    scores(i)
+                elif rank == 2:
+                    row_sum(i)
+                    pending.append((done + 1, 3, i))
+                else:
+                    finish(i)

@@ -207,9 +207,7 @@ def tile_visionattention_pa_kernel(tc, x, Wq, bq, k, out):
 
         def exponentials(i):
             nm = stat.tile([P, 1], F32, name="nmax")
-            nc.vector.tensor_scalar(
-                out=nm[:], in0=mx[i][:, 0:1], scalar1=mx[i][:, 1:2], scalar2=-1.0, op0=ALU.max, op1=ALU.mult
-            )
+            nc.vector.tensor_reduce(out=nm[:], in_=mx[i][:], axis=AX.X, op=ALU.max, negate=True)
             ex[i] = soft.tile([P, NTOK], F32, name="e")
             ssum[i] = stat.tile([P, 2], F32, name="ssum")
             for h in range(2):

from contextlib import ExitStack
import math

import concourse.mybir as mybir
from concourse.masks import make_identity

F32 = mybir.dt.float32
BF16 = mybir.dt.bfloat16
U32 = mybir.dt.uint32
U8 = mybir.dt.uint8
FP8X4 = mybir.dt.float8_e4m3fn_x4
ALU = mybir.AluOpType
ACT = mybir.ActivationFunctionType
AX = mybir.AxisListType

P = 128
C = 512
NTOK = 1024
NT = NTOK // P
QBANK = F32

FLOPS = 2 * NTOK * C * C + 2 * NTOK * NTOK * C

X_CHUNKS = (256, 256, 512)
AHEAD = 3
V_TAIL = 3


def tile_visionattention_pa_kernel(tc, x, Wq, bq, k, out):
    nc = tc.nc
    inv_sqrt_c = 1.0 / math.sqrt(C)

    with ExitStack() as ctx:
        const = ctx.enter_context(tc.tile_pool(name="const", bufs=1))
        keep = ctx.enter_context(tc.tile_pool(name="keep", bufs=1))
        soft = ctx.enter_context(tc.tile_pool(name="soft", bufs=5))
        stat = ctx.enter_context(tc.tile_pool(name="stat", bufs=6))
        psum = ctx.enter_context(tc.psum_pool(name="psum", bufs=8))
        ctx.enter_context(tc.manual_schedule())

        bq_raw = const.tile([P, 4], BF16, name="bq_raw")
        nc.scalar.dma_start(out=bq_raw[:], in_=bq.rearrange("(p t) -> p t", t=4))

        w_view = Wq.rearrange("(m t) c -> m t c", t=4)
        x_view = x[0].rearrange("(p j) h w -> p j (h w)", j=4)
        k_view = k[0].rearrange("(g r b) c -> r g b c", r=P, b=2)
        w_raw = {}
        x_raw = {}
        k_raw = {}

        def load_w(b):
            w_raw[b] = keep.tile([P, 2, C], BF16, name="w_raw%d" % b)
            nc.sync.dma_start(out=w_raw[b][:], in_=w_view[:, 2 * b : 2 * b + 2, :])

        def load_x(c):
            n0 = sum(X_CHUNKS[:c])
            x_raw[c] = keep.tile([P, 4, X_CHUNKS[c]], BF16, name="x_raw%d" % c)
            nc.sync.dma_start(out=x_raw[c][:], in_=x_view[:, :, n0 : n0 + X_CHUNKS[c]])

        def load_k(g):
            k_raw[g] = keep.tile([P, 2, C], BF16, name="k_raw%d" % g)
            nc.sync.dma_start(out=k_raw[g][:], in_=k_view[:, g, :, :])

        load_w(0)
        load_w(1)
        load_k(0)
        load_x(0)
        load_k(1)
        load_k(2)
        load_x(1)
        load_k(3)
        load_x(2)

        ident = const.tile([P, P], F32, name="ident")
        make_identity(nc, ident[:])
        warm_in = const.tile([P, 1], F32, name="warm_in")
        warm_out = const.tile([P, 1], F32, name="warm_out")
        nc.vector.memset(warm_in[:], 0.0)
        nc.scalar.activation(out=warm_out[:], in_=warm_in[:], func=ACT.Exp)
        bias_s = const.tile([P, 4], F32, name="bias_s")

        def turn(raw, name):
            words = raw[:].rearrange("r s c -> r (s c)").bitcast(F32)
            bank = psum.tile([P, 2, 2, P], F32, tag="bank", name=name)
            for s in range(2):
                for u in range(2):
                    nc.tensor.transpose(bank[:, s, u, :], words[:, 256 * s + u : 256 * (s + 1) : 2], ident[:])
            return bank

        w_grp = keep.tile([P, 4 * C], BF16, name="w_grp", align_bytes=64)
        w_codes = keep.tile([P, C], U32, name="w_codes", align_bytes=64)
        w_scales = keep.tile([P, C], U8, name="w_scales", align_bytes=64)

        def turn_w(b):
            bank = turn(w_raw[b], "wt%d" % b)
            nc.scalar.copy(
                out=w_grp[:].bitcast(F32)[:, 512 * b : 512 * (b + 1)].rearrange("p (s r u) -> p s r u", s=2, u=2),
                in_=bank[:].rearrange("p s u r -> p s r u"),
            )

        x_grp = {}
        x_codes = {}
        x_scales = {}

        def group_x(c, engine):
            x_grp[c] = keep.tile([P, X_CHUNKS[c], 4], BF16, name="x_grp%d" % c, align_bytes=64)
            src = x_raw[c][:].rearrange("p j n -> p n j")
            if engine == "scalar":
                nc.scalar.copy(out=x_grp[c][:], in_=src)
            else:
                nc.vector.tensor_copy(out=x_grp[c][:], in_=src)

        def quant_x(c):
            x_codes[c] = keep.tile([P, X_CHUNKS[c]], U32, name="x_codes%d" % c, align_bytes=64)
            x_scales[c] = keep.tile([P, X_CHUNKS[c]], U8, name="x_scales%d" % c, align_bytes=64)
            nc.vector.quantize_mx(
                out=x_codes[c][:].bitcast(FP8X4), scales=x_scales[c][:], in_=x_grp[c][:].rearrange("p n j -> p (n j)")
            )

        k_grp = {}
        for h in range(2):
            k_grp[h] = keep.tile([P, 4 * C], BF16, name="k_grp%d" % h, align_bytes=64)
        k_codes = {}
        k_scales = {}

        def turn_k(g):
            bank = turn(k_raw[g], "kt%d" % g)
            nc.scalar.copy(
                out=k_grp[g // 2][:].bitcast(F32)[:, 512 * (g % 2) : 512 * (g % 2 + 1)].rearrange("p (r q) -> p r q", q=4),
                in_=bank[:].rearrange("p b u r -> p r (b u)"),
            )

        def quant_k(h):
            k_codes[h] = keep.tile([P, C], U32, name="k_codes%d" % h, align_bytes=64)
            k_scales[h] = keep.tile([P, C], U8, name="k_scales%d" % h, align_bytes=64)
            nc.vector.quantize_mx(out=k_codes[h][:].bitcast(FP8X4), scales=k_scales[h][:], in_=k_grp[h][:])

        chunk_of = []
        for c in range(len(X_CHUNKS)):
            for j in range(X_CHUNKS[c] // P):
                chunk_of.append((c, j))

        q_bank = {}
        q_grp = {}
        q_codes = {}
        q_scales = {}

        def project(i):
            c, j = chunk_of[i]
            if c not in x_codes:
                quant_x(c)
            q_bank[i] = psum.tile([P, 4, P], QBANK, tag="bank", name="qp")
            for t in range(4):
                nc.tensor.matmul_mx(
                    out=q_bank[i][:, t, :],
                    lhsT=w_codes[:, P * t : P * (t + 1)].bitcast(FP8X4),
                    lhsT_scale=w_scales[:, P * t : P * (t + 1)],
                    rhs=x_codes[c][:, P * j : P * (j + 1)].bitcast(FP8X4),
                    rhs_scale=x_scales[c][:, P * j : P * (j + 1)],
                    start=True,
                    stop=True,
                )

        def read_q(i):
            q_grp[i] = keep.tile([P, P, 4], BF16, name="q_grp%d" % i, align_bytes=64)
            nc.vector.scalar_tensor_tensor(
                out=q_grp[i][:],
                in0=q_bank[i][:].rearrange("p t n -> p n t"),
                scalar=inv_sqrt_c,
                in1=bias_s[:].unsqueeze(1).to_broadcast([P, P, 4]),
                op0=ALU.mult,
                op1=ALU.add,
            )

        def quant_q(i):
            q_codes[i] = keep.tile([P, P], U32, name="q_codes%d" % i, align_bytes=64)
            q_scales[i] = keep.tile([P, P], U8, name="q_scales%d" % i, align_bytes=64)
            nc.vector.quantize_mx(
                out=q_codes[i][:].bitcast(FP8X4), scales=q_scales[i][:], in_=q_grp[i][:].rearrange("p n t -> p (n t)")
            )

        sc = {}
        mx = {}
        ex = {}
        ssum = {}
        tot = {}

        def scores(i):
            sc[i] = []
            for h in range(2):
                s_h = psum.tile([P, C], F32, tag="bank", name="sc%d" % h)
                nc.tensor.matmul_mx(
                    out=s_h[:],
                    lhsT=q_codes[i][:].bitcast(FP8X4),
                    lhsT_scale=q_scales[i][:],
                    rhs=k_codes[h][:].bitcast(FP8X4),
                    rhs_scale=k_scales[h][:],
                    start=True,
                    stop=True,
                )
                sc[i].append(s_h)

        def bank_max(i, h):
            if h == 0:
                mx[i] = stat.tile([P, 2], F32, name="mx")
            nc.vector.tensor_reduce(out=mx[i][:, h : h + 1], in_=sc[i][h][:], axis=AX.X, op=ALU.max)

        def exponentials(i):
            nm = stat.tile([P, 1], F32, name="nmax")
            nc.vector.tensor_reduce(out=nm[:], in_=mx[i][:], axis=AX.X, op=ALU.max, negate=True)
            ex[i] = soft.tile([P, NTOK], F32, name="e")
            ssum[i] = stat.tile([P, 2], F32, name="ssum")
            for h in range(2):
                nc.scalar.activation(
                    out=ex[i][:, C * h : C * (h + 1)],
                    in_=sc[i][h][:],
                    func=ACT.Exp,
                    bias=nm[:],
                    scale=1.0,
                    accum_out=ssum[i][:, h : h + 1],
                )

        def row_sum(i):
            tot[i] = stat.tile([P, 1], F32, name="tot")
            nc.vector.tensor_reduce(out=tot[i][:], in_=ssum[i][:], axis=AX.X, op=ALU.add)

        def finish(i):
            rinv = stat.tile([P, 1], F32, name="rinv")
            nc.vector.reciprocal(out=rinv[:], in_=tot[i][:])
            o = soft.tile([P, NTOK], F32, name="o")
            for h in range(2):
                cols = slice(C * h, C * (h + 1))
                if i >= NT - V_TAIL:
                    nc.vector.tensor_scalar(out=o[:, cols], in0=ex[i][:, cols], scalar1=rinv[:], scalar2=None, op0=ALU.mult)
                else:
                    nc.gpsimd.tensor_scalar(
                        out=o[:, cols], in0=ex[i][:, cols], scalar1=rinv[:], scalar2=0.0, op0=ALU.mult, op1=ALU.add
                    )
                nc.sync.dma_start(out=out[0, P * i : P * (i + 1), cols], in_=o[:, cols])

        turn_w(0)
        turn_w(1)
        group_x(0, "vector")
        nc.vector.quantize_mx(out=w_codes[:].bitcast(FP8X4), scales=w_scales[:], in_=w_grp[:])
        quant_x(0)
        nc.vector.tensor_scalar(out=bias_s[:], in0=bq_raw[:], scalar1=inv_sqrt_c, scalar2=None, op0=ALU.mult)
        turn_k(0)
        turn_k(1)
        turn_k(2)
        group_x(1, "scalar")
        project(0)
        quant_k(0)
        project(1)
        read_q(0)
        read_q(1)
        quant_q(0)
        quant_x(1)
        turn_k(3)
        quant_q(1)
        project(2)
        group_x(2, "scalar")
        quant_k(1)
        scores(0)
        scores(1)
        read_q(2)

        big = []
        for i in range(NT):
            big.append(("max", i, 0))
            big.append(("max", i, 1))
            if i + AHEAD < NT:
                big.append(("read_q", i + AHEAD, 0))
        pending = [(1, 1, AHEAD - 1)]
        done = 0
        while done < len(big) or pending:
            if done < len(big):
                kind, i, h = big[done]
                if kind == "max":
                    if h == 0 and i + AHEAD < NT:
                        project(i + AHEAD)
                    bank_max(i, h)
                    if h == 1:
                        pending.append((done + 2, 0, i))
                else:
                    read_q(i)
                    pending.append((done + 2, 1, i))
            done += 1
            ready = sorted(p for p in pending if p[0] <= done)
            ready = sorted(ready, key=lambda p: (p[1], p[2]))
            pending = [p for p in pending if p[0] > done]
            for due, rank, i in ready:
                if rank == 0:
                    exponentials(i)
                    pending.append((done + 3, 2, i))
                elif rank == 1:
                    quant_q(i)
                    scores(i)
                elif rank == 2:
                    row_sum(i)
                    pending.append((done + 1, 3, i))
                else:
                    finish(i)
